import numpy as np
import ml_dtypes


def mxq(x, axis, fmt="e4m3"):
    dtype, down = {"e4m3": (ml_dtypes.float8_e4m3fn, 7), "e5m2": (ml_dtypes.float8_e5m2, 14)}[fmt]
    v = np.moveaxis(np.asarray(x, np.float32).astype(ml_dtypes.bfloat16).astype(np.float64), axis, -1)
    blocks = v.reshape(v.shape[:-1] + (-1, 32))
    amax = np.abs(blocks).max(-1, keepdims=True)
    byte = np.maximum(np.where(amax > 0, np.frexp(amax)[1] - 1 + 127, 0) - down, 1)
    scale = np.exp2(byte - 127.0)
    codes = (blocks / scale).astype(np.float32).astype(dtype).astype(np.float64)
    return np.moveaxis((codes * scale).reshape(v.shape), -1, axis)


WIDE = False


def mx_kscale(k):
    if not WIDE:
        return np.ones(k)
    levels = np.array([10, -10, 5, -5, 0])
    a = np.random.permutation(np.resize(levels, k // 512 * 4)).reshape(k // 512, 4)
    idx = np.arange(k)
    return np.exp2(a[idx // 512, idx % 128 // 32])


BF16 = ml_dtypes.bfloat16


def bf(x):
    return np.asarray(x, np.float32).astype(BF16)


def f64(x):
    return np.asarray(x).astype(np.float64)


B, Q, K, D = 2, 512, 1024, 1024
C = D + D


def setup_inputs():
    s, t = mx_kscale(K), mx_kscale(C)
    z = np.exp(2.0 * np.random.standard_normal((B, Q, K)))
    return {"attn_weights": bf(z / z.sum(-1, keepdims=True) * s),
            "context": bf(np.random.standard_normal((B, K, D)) * 0.5 / s[:, None] * t[:D]),
            "q": bf(np.random.standard_normal((B, Q, D)) * 4.0 / np.sqrt(D) * t[D:]),
            "W_out": bf(np.random.standard_normal((D, C)) * 6.0 / np.sqrt(C) / t),
            "b_out": bf(np.random.standard_normal(D) * 0.2)}


def reference(attn_weights, context, q, W_out, b_out):
    mix = mxq(f64(attn_weights), 2, "e4m3") @ mxq(f64(context), 1, "e4m3")
    combined = np.concatenate([mix, f64(q)], axis=-1)
    return np.tanh((mxq(combined, 2, "e4m3") @ mxq(f64(W_out), 1, "e4m3").T) + f64(b_out))

@@ -1,0 +1,309 @@
+from contextlib import ExitStack
+
+import concourse.mybir as mybir
+from concourse.masks import make_identity
+
+F32 = mybir.dt.float32
+BF16 = mybir.dt.bfloat16
+U32 = mybir.dt.uint32
+U8 = mybir.dt.uint8
+FP8X4 = mybir.dt.float8_e4m3fn_x4
+TANH = mybir.ActivationFunctionType.Tanh
+ADD = mybir.AluOpType.add
+
+P = 128
+FLOPS = 2 * 2 * 512 * 1024 * 1024 + 2 * 2 * 512 * 2048 * 1024
+
+
+def tile_attention_pb_kernel(tc, attn_weights, context, q, W_out, b_out, out):
+    nc = tc.nc
+    with ExitStack() as ctx:
+        ctx.enter_context(tc.manual_schedule())
+        const = ctx.enter_context(tc.tile_pool(name="const", bufs=1))
+        raw = ctx.enter_context(tc.tile_pool(name="raw", bufs=9))
+        grp = ctx.enter_context(tc.tile_pool(name="grp", bufs=2))
+        keep = ctx.enter_context(tc.tile_pool(name="keep", bufs=1))
+        res = ctx.enter_context(tc.tile_pool(name="res", bufs=4))
+        ps_a = ctx.enter_context(tc.psum_pool(name="ps_a", bufs=4))
+        ps_2 = ctx.enter_context(tc.psum_pool(name="ps_2", bufs=4))
+
+        ident = const.tile([P, P], F32, name="ident")
+        make_identity(nc, ident[:])
+        ones = const.tile([P, P], BF16, name="ones")
+        nc.vector.memset(ones[:], 1.0)
+        brow = const.tile([P, 1024], BF16, name="brow")
+        nc.vector.memset(brow[:], 0.0)
+        warm = const.tile([P, 8], F32, name="warm")
+        nc.vector.memset(warm[:], 0.0)
+        nc.scalar.activation(out=warm[:], in_=warm[:], func=TANH)
+        bias = const.tile([P, 1024], F32, name="bias")
+
+        def codes(name, width):
+            c = keep.tile([P, width], U32, name=name + "_c", align_bytes=64)
+            s = keep.tile([P, width], U8, name=name + "_s", align_bytes=64)
+            return c, s
+
+        a_q = [codes("a%d" % b, 1024) for b in range(2)]
+        c_q = [codes("c%d" % b, 2048) for b in range(2)]
+        q_q = [codes("q%d" % b, 1024) for b in range(2)]
+        m_q = [codes("m%d" % b, 1024) for b in range(2)]
+        w_q = codes("w", 4096)
+
+        def quantise(dst, lo, src):
+            n = src.shape[1] // 4
+            nc.vector.quantize_mx(out=dst[0][:, lo:lo + n].bitcast(FP8X4), scales=dst[1][:, lo:lo + n], in_=src)
+
+        raws = {}
+        banks = {}
+        g_tiles = {}
+
+        def new_raw(key):
+            raws[key] = raw.tile([P, 4096], BF16, name="raw_" + key, tag="raw")
+            return raws[key]
+
+        def load_rows(key, src, j):
+            if j == 0:
+                new_raw(key)
+            w = 4096 // 2
+            nc.sync.dma_start(out=raws[key][:, j * w:(j + 1) * w].rearrange("p (r c) -> p r c", r=2),
+                              in_=src[j * 256:(j + 1) * 256, :].rearrange("(r p) c -> p r c", p=P))
+
+        def load_w(pair):
+            t = new_raw("w%d" % pair)
+            nc.sync.dma_start(out=t[:].rearrange("p (r c) -> p r c", r=2),
+                              in_=W_out[pair * 256:(pair + 1) * 256, :].rearrange("(r p) c -> p r c", p=P))
+
+        def load_c_split(b, G, g):
+            if g == 0:
+                new_raw("c%d%d" % (b, G))
+            t = raws["c%d%d" % (b, G)]
+            for u in range(2):
+                gu = 2 * g + u
+                nc.sync.dma_start(
+                    out=t[:, gu * 1024:(gu + 1) * 1024].rearrange("p (e f) -> p e f", e=2),
+                    in_=context[b, gu * 256:(gu + 1) * 256, G * 512:(G + 1) * 512].rearrange("(p e) f -> p e f", e=2))
+
+        def load_c_rows(b, g):
+            t = new_raw("c%d%d" % (b, g))
+            nc.sync.dma_start(out=t[:].rearrange("p (u x) -> p u x", u=2),
+                              in_=context[b, g * 512:(g + 1) * 512, :].rearrange("(u p e) f -> p u (e f)", u=2, e=2))
+
+        def c_src(b, g, G):
+            if b == 0:
+                return raws["c%d%d" % (b, G)][:].rearrange("p (g t f) -> p g t f", g=2, t=4)[:, g]
+            return raws["c%d%d" % (b, g)][:].rearrange("p (t f) -> p t f", t=4)[:, :, G * 512:(G + 1) * 512]
+
+        def pe_transposes(key, words, cols):
+            bank = ps_a.tile([P, 512], F32, name="tp", tag="a")
+            banks[key] = bank
+            for i, c0 in enumerate(cols):
+                nc.tensor.transpose(out=bank[:, i * P:(i + 1) * P], in_=words[:, c0:c0 + P], identity=ident[:])
+
+        def pe_T_rows(kind, b, qb):
+            pe_transposes((kind, b, qb), raws["%s%d" % (kind, b)][:].bitcast(F32), [qb * 512 + i * P for i in range(4)])
+
+        def pe_T_w(pair, Pp):
+            pe_transposes(("w", pair, Pp), raws["w%d" % pair][:].bitcast(F32),
+                          [h * 1024 + Pp * 256 + u * P for h in range(2) for u in range(2)])
+
+        def pe_S1(b, G, qb):
+            bank = ps_a.tile([P, 512], F32, name="s1", tag="a")
+            banks["m", b, G, qb] = bank
+            for t2 in range(4):
+                for g in range(2):
+                    lo = g * 1024 + (4 * G + t2) * P
+                    ro = (qb * 2 + g) * P
+                    nc.tensor.matmul_mx(out=bank[:, t2 * P:(t2 + 1) * P],
+                                        lhsT=c_q[b][0][:, lo:lo + P].bitcast(FP8X4), lhsT_scale=c_q[b][1][:, lo:lo + P],
+                                        rhs=a_q[b][0][:, ro:ro + P].bitcast(FP8X4), rhs_scale=a_q[b][1][:, ro:ro + P],
+                                        start=(g == 0), stop=(g == 1))
+
+        def pe_S2(b, qb, pair):
+            oh, pr = pair // 2, pair % 2
+            if pr == 0:
+                banks["o", b, qb, oh] = ps_2.tile([P, 512], F32, name="s2", tag="s2")
+            bank = banks["o", b, qb, oh]
+            for i, Pp in enumerate((2, 3, 0, 1)):
+                if Pp < 2:
+                    lc, lo = m_q[b], Pp * 512 + qb * P
+                else:
+                    lc, lo = q_q[b], (qb * 2 + Pp - 2) * P
+                ro = pair * 1024 + Pp * 256
+                nc.tensor.matmul_mx(out=bank[:, pr * 256:(pr + 1) * 256],
+                                    lhsT=lc[0][:, lo:lo + P].bitcast(FP8X4), lhsT_scale=lc[1][:, lo:lo + P],
+                                    rhs=w_q[0][:, ro:ro + 256].bitcast(FP8X4), rhs_scale=w_q[1][:, ro:ro + 256],
+                                    start=(i == 0), stop=(i == 3))
+
+        def cp(eng):
+            return nc.scalar.copy if eng == "s" else nc.vector.tensor_copy
+
+        def g_half(key, tag, bufs, half):
+            if half == 0:
+                g_tiles[key] = grp.tile([P, 2048], BF16, name="g" + tag, tag=tag, bufs=bufs, align_bytes=64)
+            return g_tiles[key][:, half * 1024:(half + 1) * 1024]
+
+        def cp_words(eng, dst, bank):
+            cp(eng)(out=dst.bitcast(F32).rearrange("p (x r u) -> p x r u", x=2, u=2),
+                    in_=bank[:].rearrange("p (x u r) -> p x r u", x=2, u=2))
+
+        def cp_rows(eng, kind, b, qb):
+            cp_words(eng, g_half((kind, b, qb // 2), "ga", 3, qb % 2), banks[kind, b, qb])
+
+        def cp_w(eng, pair, Pp):
+            cp_words(eng, g_half(("w", pair, Pp // 2), "gw", 3, Pp % 2), banks["w", pair, Pp])
+
+        def cp_m(eng, b, G, qb):
+            if qb == 0:
+                g_tiles["m", b, G] = grp.tile([P, 2048], BF16, name="gm", tag="gm", bufs=2, align_bytes=64)
+            cp(eng)(out=g_tiles["m", b, G][:, qb * 512:(qb + 1) * 512].rearrange("p (q t) -> p q t", t=4),
+                    in_=banks["m", b, G, qb][:].rearrange("p (t q) -> p q t", t=4))
+
+        def R_c(eng, b, g, G, ef):
+            if ("c", b, g, G) not in g_tiles:
+                g_tiles["c", b, g, G] = grp.tile([P, 2048], BF16, name="gc", tag="gc", bufs=4, align_bytes=64)
+            gt = g_tiles["c", b, g, G]
+            src = c_src(b, g, G)
+            if eng == "s":
+                nc.scalar.copy(out=gt[:].rearrange("p (J ef pp t) -> p J ef pp t", J=2, ef=2, t=4)[:, :, ef],
+                               in_=src.rearrange("p t (J pp ef) -> p J ef pp t", J=2, ef=2)[:, :, ef])
+            else:
+                nc.vector.tensor_copy(out=gt[:].rearrange("p (J ef c i t) -> p J ef c t i", J=2, ef=2, i=4, t=4)[:, :, ef],
+                                      in_=src.rearrange("p t (J c i ef) -> p J ef c t i", J=2, i=4, ef=2)[:, :, ef])
+
+        def Q_rows(kind, b, j):
+            quantise(a_q[b] if kind == "a" else q_q[b], j * 512, g_tiles[kind, b, j][:])
+
+        def Q_w(pair, half):
+            quantise(w_q, pair * 1024 + half * 512, g_tiles["w", pair, half][:])
+
+        def Q_c(b, g, G):
+            quantise(c_q[b], g * 1024 + G * 512, g_tiles["c", b, g, G][:])
+
+        def Q_m(b, G):
+            quantise(m_q[b], G * 512, g_tiles["m", b, G][:])
+
+        pres = {}
+
+        def v_add(b, qb, oh):
+            pres[b, qb, oh] = res.tile([P, 512], F32, name="pre", tag="pre")
+            nc.vector.tensor_tensor(out=pres[b, qb, oh][:], in0=banks["o", b, qb, oh][:],
+                                    in1=bias[:, oh * 512:(oh + 1) * 512], op=ADD)
+
+        def s_tanh(b, qb, oh):
+            fin = res.tile([P, 512], F32, name="fin", tag="fin")
+            nc.scalar.activation(out=fin[:], in_=pres[b, qb, oh][:], func=TANH)
+            nc.sync.dma_start(out=out[b, qb * P:(qb + 1) * P, oh * 512:(oh + 1) * 512], in_=fin[:])
+
+        nc.sync.dma_start(out=brow[0:1, :], in_=b_out.rearrange("(o n) -> o n", o=1))
+        load_c_split(0, 0, 0)
+        load_rows("a0", attn_weights[0], 0)
+        load_c_split(0, 0, 1)
+        load_rows("a0", attn_weights[0], 1)
+        load_c_split(0, 1, 0)
+        load_c_split(0, 1, 1)
+        load_rows("q0", q[0], 0)
+        load_rows("q0", q[0], 1)
+        load_w(0)
+        load_c_rows(1, 0)
+        load_w(1)
+        load_c_rows(1, 1)
+        load_w(2)
+
+        for oh in range(2):
+            bb = ps_2.tile([P, 512], F32, name="bb", tag="s2")
+            nc.tensor.matmul(out=bb[:], lhsT=ones[:], rhs=brow[:, oh * 512:(oh + 1) * 512], start=True, stop=True)
+            nc.scalar.copy(out=bias[:, oh * 512:(oh + 1) * 512], in_=bb[:])
+        R_c("v", 0, 0, 0, 0)
+        R_c("v", 0, 0, 0, 1)
+        for qb in range(2):
+            pe_T_rows("a", 0, qb)
+            cp_rows("s", "a", 0, qb)
+        Q_c(0, 0, 0)
+        Q_rows("a", 0, 0)
+        R_c("v", 0, 1, 0, 0)
+        R_c("s", 0, 1, 0, 1)
+        for qb in range(2, 4):
+            pe_T_rows("a", 0, qb)
+            cp_rows("s", "a", 0, qb)
+        Q_c(0, 1, 0)
+        Q_rows("a", 0, 1)
+        load_w(3)
+        R_c("v", 0, 0, 1, 0)
+        R_c("v", 0, 0, 1, 1)
+        R_c("s", 0, 1, 1, 1)
+        Q_c(0, 0, 1)
+        R_c("v", 0, 1, 1, 0)
+        Q_c(0, 1, 1)
+        load_rows("a1", attn_weights[1], 0)
+        load_rows("a1", attn_weights[1], 1)
+        load_rows("q1", q[1], 0)
+        load_rows("q1", q[1], 1)
+
+        for qb in range(4):
+            pe_S1(0, 0, qb)
+            cp_m("s" if qb != 1 else "v", 0, 0, qb)
+        Q_m(0, 0)
+        for qb in range(4):
+            pe_T_rows("q", 0, qb)
+            cp_rows("s", "q", 0, qb)
+            if qb % 2 == 1:
+                Q_rows("q", 0, qb // 2)
+        for qb in range(4):
+            pe_S1(0, 1, qb)
+            cp_m("s" if qb % 2 == 0 else "v", 0, 1, qb)
+        Q_m(0, 1)
+        for Pp in range(4):
+            pe_T_w(0, Pp)
+            cp_w("s", 0, Pp)
+            if Pp % 2 == 1:
+                Q_w(0, Pp // 2)
+        R_c("v", 1, 0, 0, 0); R_c("v", 1, 0, 0, 1);
+        R_c("v", 1, 0, 1, 0); R_c("v", 1, 0, 1, 1); Q_c(1, 0, 0); Q_c(1, 0, 1)
+
+        for pair in range(4):
+            if pair % 2 == 0 and pair > 0:
+                for qb in range(2):
+                    s_tanh(0, qb, pair // 2 - 1)
+            for i in range(4):
+                if pair < 3:
+                    pe_T_w(pair + 1, i)
+                    cp_w("s", pair + 1, i)
+                    if i % 2 == 1:
+                        Q_w(pair + 1, i // 2)
+                else:
+                    pe_T_rows("a", 1, i)
+                    cp_rows("s", "a", 1, i)
+                    if i % 2 == 1:
+                        Q_rows("a", 1, i // 2)
+            if pair % 2 == 0 and pair > 0:
+                for qb in range(2, 4):
+                    s_tanh(0, qb, pair // 2 - 1)
+            for qb in range(4):
+                pe_S2(0, qb, pair)
+                if pair % 2 == 1:
+                    v_add(0, qb, pair // 2)
+            if pair == 0:
+                R_c("v", 1, 1, 0, 0); R_c("v", 1, 1, 0, 1);
+                R_c("v", 1, 1, 1, 0); R_c("v", 1, 1, 1, 1); Q_c(1, 1, 0);Q_c(1, 1, 1)
+
+        for qb in range(4):
+            pe_S1(1, 0, qb)
+            cp_m("s" if qb % 2 == 0 else "v", 1, 0, qb)
+            s_tanh(0, qb, 1)
+        Q_m(1, 0)
+        for qb in range(4):
+            pe_T_rows("q", 1, qb)
+            cp_rows("s" if qb % 2 == 0 else "v", "q", 1, qb)
+            if qb % 2 == 1:
+                Q_rows("q", 1, qb // 2)
+        for qb in range(4):
+            pe_S1(1, 1, qb)
+            cp_m("s" if qb % 2 == 0 else "v", 1, 1, qb)
+        Q_m(1, 1)
+
+        for qb in range(4):
+            for oh in range(2):
+                pe_S2(1, qb, 2 * oh)
+                pe_S2(1, qb, 2 * oh + 1)
+                v_add(1, qb, oh)
+                s_tanh(1, qb, oh)

@@ -61,12 +61,11 @@ def tile_attention_pb_kernel(tc, attn_weights, context, q, W_out, b_out, out):
             raws[key] = raw.tile([P, 4096], BF16, name="raw_" + key, tag="raw")
             return raws[key]
 
-        def load_rows(key, src, j):
-            if j == 0:
+        def load_rows(key, src, first, blocks):
+            if first == 0:
                 new_raw(key)
-            w = 4096 // 2
-            nc.sync.dma_start(out=raws[key][:, j * w:(j + 1) * w].rearrange("p (r c) -> p r c", r=2),
-                              in_=src[j * 256:(j + 1) * 256, :].rearrange("(r p) c -> p r c", p=P))
+            nc.sync.dma_start(out=raws[key][:, first * 1024:(first + blocks) * 1024].rearrange("p (r c) -> p r c", r=blocks),
+                              in_=src[first * P:(first + blocks) * P, :].rearrange("(r p) c -> p r c", p=P))
 
         def load_w(pair):
             t = new_raw("w%d" % pair)
@@ -125,7 +124,7 @@ def tile_attention_pb_kernel(tc, attn_weights, context, q, W_out, b_out, out):
             bank = banks["o", b, qb, oh]
             for i, Pp in enumerate((2, 3, 0, 1)):
                 if Pp < 2:
-                    lc, lo = m_q[b], Pp * 512 + qb * P
+                    lc, lo = m_q[b], (qb * 2 + Pp) * P
                 else:
                     lc, lo = q_q[b], (qb * 2 + Pp - 2) * P
                 ro = pair * 1024 + Pp * 256
@@ -142,20 +141,24 @@ def tile_attention_pb_kernel(tc, attn_weights, context, q, W_out, b_out, out):
                 g_tiles[key] = grp.tile([P, 2048], BF16, name="g" + tag, tag=tag, bufs=bufs, align_bytes=64)
             return g_tiles[key][:, half * 1024:(half + 1) * 1024]
 
+        def g_new(key, tag, bufs):
+            g_tiles[key] = grp.tile([P, 1024], BF16, name="g" + tag, tag=tag, bufs=bufs, align_bytes=64)
+            return g_tiles[key]
+
         def cp_words(eng, dst, bank):
             cp(eng)(out=dst.bitcast(F32).rearrange("p (x r u) -> p x r u", x=2, u=2),
                     in_=bank[:].rearrange("p (x u r) -> p x r u", x=2, u=2))
 
         def cp_rows(eng, kind, b, qb):
-            cp_words(eng, g_half((kind, b, qb // 2), "ga", 3, qb % 2), banks[kind, b, qb])
+            cp_words(eng, g_new((kind, b, qb), "ga", 4)[:], banks[kind, b, qb])
 
         def cp_w(eng, pair, Pp):
-            cp_words(eng, g_half(("w", pair, Pp // 2), "gw", 3, Pp % 2), banks["w", pair, Pp])
+            cp_words(eng, g_half(("w", pair, Pp // 2), "gw", 4, Pp % 2), banks["w", pair, Pp])
 
         def cp_m(eng, b, G, qb):
-            if qb == 0:
-                g_tiles["m", b, G] = grp.tile([P, 2048], BF16, name="gm", tag="gm", bufs=2, align_bytes=64)
-            cp(eng)(out=g_tiles["m", b, G][:, qb * 512:(qb + 1) * 512].rearrange("p (q t) -> p q t", t=4),
+            if G == 0:
+                g_new(("m", b, qb), "gm", 4)
+            cp(eng)(out=g_tiles["m", b, qb][:, G * 512:(G + 1) * 512].rearrange("p (q t) -> p q t", t=4),
                     in_=banks["m", b, G, qb][:].rearrange("p (t q) -> p q t", t=4))
 
         def R_c(eng, b, g, G, ef):
@@ -170,8 +173,8 @@ def tile_attention_pb_kernel(tc, attn_weights, context, q, W_out, b_out, out):
                 nc.vector.tensor_copy(out=gt[:].rearrange("p (J ef c i t) -> p J ef c t i", J=2, ef=2, i=4, t=4)[:, :, ef],
                                       in_=src.rearrange("p t (J c i ef) -> p J ef c t i", J=2, i=4, ef=2)[:, :, ef])
 
-        def Q_rows(kind, b, j):
-            quantise(a_q[b] if kind == "a" else q_q[b], j * 512, g_tiles[kind, b, j][:])
+        def Q_rows(kind, b, qb):
+            quantise(a_q[b] if kind == "a" else q_q[b], qb * 256, g_tiles[kind, b, qb][:])
 
         def Q_w(pair, half):
             quantise(w_q, pair * 1024 + half * 512, g_tiles["w", pair, half][:])
@@ -179,8 +182,8 @@ def tile_attention_pb_kernel(tc, attn_weights, context, q, W_out, b_out, out):
         def Q_c(b, g, G):
             quantise(c_q[b], g * 1024 + G * 512, g_tiles["c", b, g, G][:])
 
-        def Q_m(b, G):
-            quantise(m_q[b], G * 512, g_tiles["m", b, G][:])
+        def Q_m(b, qb):
+            quantise(m_q[b], qb * 256, g_tiles["m", b, qb][:])
 
         pres = {}
 
@@ -195,115 +198,132 @@ def tile_attention_pb_kernel(tc, attn_weights, context, q, W_out, b_out, out):
             nc.sync.dma_start(out=out[b, qb * P:(qb + 1) * P, oh * 512:(oh + 1) * 512], in_=fin[:])
 
         nc.sync.dma_start(out=brow[0:1, :], in_=b_out.rearrange("(o n) -> o n", o=1))
+        load_rows("a0", attn_weights[0], 0, 1)
         load_c_split(0, 0, 0)
-        load_rows("a0", attn_weights[0], 0)
         load_c_split(0, 0, 1)
-        load_rows("a0", attn_weights[0], 1)
+        load_rows("a0", attn_weights[0], 1, 1)
+        load_rows("a0", attn_weights[0], 2, 2)
         load_c_split(0, 1, 0)
         load_c_split(0, 1, 1)
-        load_rows("q0", q[0], 0)
-        load_rows("q0", q[0], 1)
+        load_rows("q0", q[0], 0, 2)
+        load_rows("q0", q[0], 2, 2)
         load_w(0)
-        load_c_rows(1, 0)
         load_w(1)
-        load_c_rows(1, 1)
         load_w(2)
+        load_c_rows(1, 0)
+        load_w(3)
+
+        def T_rows(eng, kind, b, qb):
+            pe_T_rows(kind, b, qb)
+            cp_rows(eng, kind, b, qb)
+
+        def T_w(eng, pair, Pp):
+            pe_T_w(pair, Pp)
+            cp_w(eng, pair, Pp)
+
+        def S1(eng, b, G, qb):
+            pe_S1(b, G, qb)
+            cp_m(eng, b, G, qb)
+
+        def ctx1(g, step):
+            if step < 4:
+                R_c("vs"[step % 2], 1, g, step // 2, step % 2)
+            else:
+                Q_c(1, g, step - 4)
 
         for oh in range(2):
             bb = ps_2.tile([P, 512], F32, name="bb", tag="s2")
             nc.tensor.matmul(out=bb[:], lhsT=ones[:], rhs=brow[:, oh * 512:(oh + 1) * 512], start=True, stop=True)
             nc.scalar.copy(out=bias[:, oh * 512:(oh + 1) * 512], in_=bb[:])
-        R_c("v", 0, 0, 0, 0)
-        R_c("v", 0, 0, 0, 1)
-        for qb in range(2):
-            pe_T_rows("a", 0, qb)
-            cp_rows("s", "a", 0, qb)
-        Q_c(0, 0, 0)
+        T_rows("s", "a", 0, 0)
+        for g in range(2):
+            R_c("v", 0, g, 0, 0)
+            R_c("s", 0, g, 0, 1)
         Q_rows("a", 0, 0)
-        R_c("v", 0, 1, 0, 0)
-        R_c("s", 0, 1, 0, 1)
-        for qb in range(2, 4):
-            pe_T_rows("a", 0, qb)
-            cp_rows("s", "a", 0, qb)
+        Q_c(0, 0, 0)
         Q_c(0, 1, 0)
+        for qb in range(1, 4):
+            T_rows("s", "a", 0, qb)
+        load_c_rows(1, 1)
         Q_rows("a", 0, 1)
-        load_w(3)
+        load_rows("a1", attn_weights[1], 0, 2)
+        load_rows("a1", attn_weights[1], 2, 2)
+        Q_rows("a", 0, 2)
         R_c("v", 0, 0, 1, 0)
+        Q_rows("a", 0, 3)
         R_c("v", 0, 0, 1, 1)
-        R_c("s", 0, 1, 1, 1)
-        Q_c(0, 0, 1)
         R_c("v", 0, 1, 1, 0)
+        R_c("v", 0, 1, 1, 1)
+        Q_c(0, 0, 1)
         Q_c(0, 1, 1)
-        load_rows("a1", attn_weights[1], 0)
-        load_rows("a1", attn_weights[1], 1)
-        load_rows("q1", q[1], 0)
-        load_rows("q1", q[1], 1)
+        load_rows("q1", q[1], 0, 2)
+        load_rows("q1", q[1], 2, 2)
 
         for qb in range(4):
-            pe_S1(0, 0, qb)
-            cp_m("s" if qb != 1 else "v", 0, 0, qb)
-        Q_m(0, 0)
+            S1("s", 0, 0, qb)
         for qb in range(4):
-            pe_T_rows("q", 0, qb)
-            cp_rows("s", "q", 0, qb)
-            if qb % 2 == 1:
-                Q_rows("q", 0, qb // 2)
+            T_rows("s", "q", 0, qb)
         for qb in range(4):
-            pe_S1(0, 1, qb)
-            cp_m("s" if qb % 2 == 0 else "v", 0, 1, qb)
-        Q_m(0, 1)
-        for Pp in range(4):
-            pe_T_w(0, Pp)
-            cp_w("s", 0, Pp)
-            if Pp % 2 == 1:
-                Q_w(0, Pp // 2)
-        R_c("v", 1, 0, 0, 0); R_c("v", 1, 0, 0, 1);
-        R_c("v", 1, 0, 1, 0); R_c("v", 1, 0, 1, 1); Q_c(1, 0, 0); Q_c(1, 0, 1)
+            Q_rows("q", 0, qb)
+        for qb in range(4):
+            S1("s", 0, 1, qb)
+        for qb in range(4):
+            Q_m(0, qb)
+        for pair in range(2):
+            for Pp in range(4):
+                T_w("sv"[Pp % 2], pair, Pp)
+                if Pp % 2 == 1:
+                    Q_w(pair, Pp // 2)
 
         for pair in range(4):
-            if pair % 2 == 0 and pair > 0:
-                for qb in range(2):
-                    s_tanh(0, qb, pair // 2 - 1)
-            for i in range(4):
-                if pair < 3:
-                    pe_T_w(pair + 1, i)
-                    cp_w("s", pair + 1, i)
-                    if i % 2 == 1:
-                        Q_w(pair + 1, i // 2)
-                else:
-                    pe_T_rows("a", 1, i)
-                    cp_rows("s", "a", 1, i)
-                    if i % 2 == 1:
-                        Q_rows("a", 1, i // 2)
-            if pair % 2 == 0 and pair > 0:
-                for qb in range(2, 4):
-                    s_tanh(0, qb, pair // 2 - 1)
             for qb in range(4):
                 pe_S2(0, qb, pair)
                 if pair % 2 == 1:
                     v_add(0, qb, pair // 2)
-            if pair == 0:
-                R_c("v", 1, 1, 0, 0); R_c("v", 1, 1, 0, 1);
-                R_c("v", 1, 1, 1, 0); R_c("v", 1, 1, 1, 1); Q_c(1, 1, 0);Q_c(1, 1, 1)
+            if pair < 2:
+                for step in range(4):
+                    ctx1(pair, step)
+                for Pp in range(4):
+                    T_w("s", pair + 2, Pp)
+                Q_w(pair + 2, 0)
+                Q_w(pair + 2, 1)
+                ctx1(pair, 4)
+                ctx1(pair, 5)
+            if pair == 1:
+                for qb in range(4):
+                    s_tanh(0, qb, 0)
+            if pair == 2:
+                for qb in range(2):
+                    T_rows("s", "a", 1, qb)
+                    T_rows("s", "q", 1, qb)
+                    Q_rows("a", 1, qb)
+                    Q_rows("q", 1, qb)
 
-        for qb in range(4):
-            pe_S1(1, 0, qb)
-            cp_m("s" if qb % 2 == 0 else "v", 1, 0, qb)
-            s_tanh(0, qb, 1)
-        Q_m(1, 0)
-        for qb in range(4):
-            pe_T_rows("q", 1, qb)
-            cp_rows("s" if qb % 2 == 0 else "v", "q", 1, qb)
-            if qb % 2 == 1:
-                Q_rows("q", 1, qb // 2)
-        for qb in range(4):
-            pe_S1(1, 1, qb)
-            cp_m("s" if qb % 2 == 0 else "v", 1, 1, qb)
-        Q_m(1, 1)
+        def A(qb):
+            T_rows("s", "a", 1, qb)
+            T_rows("s", "q", 1, qb)
+            Q_rows("a", 1, qb)
+            Q_rows("q", 1, qb)
 
+        def B(qb):
+            S1("s", 1, 0, qb)
+            S1("v", 1, 1, qb)
+            Q_m(1, qb)
+
+        B(0)
         for qb in range(4):
+            if qb + 2 < 4:
+                A(qb + 2)
+            if qb + 1 < 4:
+                B(qb + 1)
+            for i in range(4 if qb == 0 else 2):
+                if qb == 0:
+                    s_tanh(0, i, 1)
+                else:
+                    s_tanh(1, qb - 1, i)
             for oh in range(2):
                 pe_S2(1, qb, 2 * oh)
                 pe_S2(1, qb, 2 * oh + 1)
                 v_add(1, qb, oh)
-                s_tanh(1, qb, oh)
+        for oh in range(2):
+            s_tanh(1, 3, oh)

@@ -23,9 +23,9 @@ def tile_attention_pb_kernel(tc, attn_weights, context, q, W_out, b_out, out):
         raw = ctx.enter_context(tc.tile_pool(name="raw", bufs=9))
         grp = ctx.enter_context(tc.tile_pool(name="grp", bufs=2))
         keep = ctx.enter_context(tc.tile_pool(name="keep", bufs=1))
-        res = ctx.enter_context(tc.tile_pool(name="res", bufs=4))
-        ps_a = ctx.enter_context(tc.psum_pool(name="ps_a", bufs=4))
-        ps_2 = ctx.enter_context(tc.psum_pool(name="ps_2", bufs=4))
+        res = ctx.enter_context(tc.tile_pool(name="res", bufs=11))
+        ps_a = ctx.enter_context(tc.psum_pool(name="ps_a", bufs=5))
+        ps_2 = ctx.enter_context(tc.psum_pool(name="ps_2", bufs=3))
 
         ident = const.tile([P, P], F32, name="ident")
         make_identity(nc, ident[:])
@@ -117,21 +117,36 @@ def tile_attention_pb_kernel(tc, attn_weights, context, q, W_out, b_out, out):
                                         rhs=a_q[b][0][:, ro:ro + P].bitcast(FP8X4), rhs_scale=a_q[b][1][:, ro:ro + P],
                                         start=(g == 0), stop=(g == 1))
 
-        def pe_S2(b, qb, pair):
-            oh, pr = pair // 2, pair % 2
-            if pr == 0:
-                banks["o", b, qb, oh] = ps_2.tile([P, 512], F32, name="s2", tag="s2")
-            bank = banks["o", b, qb, oh]
-            for i, Pp in enumerate((2, 3, 0, 1)):
-                if Pp < 2:
-                    lc, lo = m_q[b], (qb * 2 + Pp) * P
-                else:
-                    lc, lo = q_q[b], (qb * 2 + Pp - 2) * P
-                ro = pair * 1024 + Pp * 256
-                nc.tensor.matmul_mx(out=bank[:, pr * 256:(pr + 1) * 256],
-                                    lhsT=lc[0][:, lo:lo + P].bitcast(FP8X4), lhsT_scale=lc[1][:, lo:lo + P],
-                                    rhs=w_q[0][:, ro:ro + 256].bitcast(FP8X4), rhs_scale=w_q[1][:, ro:ro + 256],
-                                    start=(i == 0), stop=(i == 3))
+        def pe_S2(b, qb, pairs):
+            bank = ps_2.tile([P, 512], F32, name="s2", tag="s2")
+            banks["o", b, qb, pairs[0]] = bank
+            for j, pair in enumerate(pairs):
+                for i, Pp in enumerate((2, 3, 0, 1)):
+                    if Pp < 2:
+                        lc, lo = m_q[b], (qb * 2 + Pp) * P
+                    else:
+                        lc, lo = q_q[b], (qb * 2 + Pp - 2) * P
+                    ro = pair * 1024 + Pp * 256
+                    nc.tensor.matmul_mx(out=bank[:, j * 256:(j + 1) * 256],
+                                        lhsT=lc[0][:, lo:lo + P].bitcast(FP8X4), lhsT_scale=lc[1][:, lo:lo + P],
+                                        rhs=w_q[0][:, ro:ro + 256].bitcast(FP8X4), rhs_scale=w_q[1][:, ro:ro + 256],
+                                        start=(i == 0), stop=(i == 3))
+
+        def pe_S2u(b, qp, pair):
+            bank = ps_2.tile([P, 512], F32, name="s2", tag="s2")
+            banks["u", b, qp, pair] = bank
+            for u in range(2):
+                qb = 2 * qp + u
+                for i, Pp in enumerate((2, 3, 0, 1)):
+                    if Pp < 2:
+                        lc, lo = m_q[b], (qb * 2 + Pp) * P
+                    else:
+                        lc, lo = q_q[b], (qb * 2 + Pp - 2) * P
+                    ro = pair * 1024 + Pp * 256
+                    nc.tensor.matmul_mx(out=bank[:, u * 256:(u + 1) * 256],
+                                        lhsT=lc[0][:, lo:lo + P].bitcast(FP8X4), lhsT_scale=lc[1][:, lo:lo + P],
+                                        rhs=w_q[0][:, ro:ro + 256].bitcast(FP8X4), rhs_scale=w_q[1][:, ro:ro + 256],
+                                        start=(i == 0), stop=(i == 3))
 
         def cp(eng):
             return nc.scalar.copy if eng == "s" else nc.vector.tensor_copy
@@ -187,15 +202,31 @@ def tile_attention_pb_kernel(tc, attn_weights, context, q, W_out, b_out, out):
 
         pres = {}
 
-        def v_add(b, qb, oh):
-            pres[b, qb, oh] = res.tile([P, 512], F32, name="pre", tag="pre")
-            nc.vector.tensor_tensor(out=pres[b, qb, oh][:], in0=banks["o", b, qb, oh][:],
-                                    in1=bias[:, oh * 512:(oh + 1) * 512], op=ADD)
+        def v_add(b, qb, pairs):
+            n = 256 * len(pairs)
+            lo = 256 * pairs[0]
+            pres[b, qb, pairs[0]] = res.tile([P, 512], F32, name="pre", tag="pre")
+            nc.vector.tensor_tensor(out=pres[b, qb, pairs[0]][:, 0:n], in0=banks["o", b, qb, pairs[0]][:, 0:n],
+                                    in1=bias[:, lo:lo + n], op=ADD)
 
-        def s_tanh(b, qb, oh):
-            fin = res.tile([P, 512], F32, name="fin", tag="fin")
-            nc.scalar.activation(out=fin[:], in_=pres[b, qb, oh][:], func=TANH)
-            nc.sync.dma_start(out=out[b, qb * P:(qb + 1) * P, oh * 512:(oh + 1) * 512], in_=fin[:])
+        def v_add_u(b, qp, pair):
+            pres["u", b, qp, pair] = res.tile([P, 512], F32, name="pre", tag="pre")
+            nc.vector.tensor_tensor(out=pres["u", b, qp, pair][:].rearrange("p (u c) -> p u c", u=2),
+                                    in0=banks["u", b, qp, pair][:].rearrange("p (u c) -> p u c", u=2),
+                                    in1=bias[:, pair * 256:(pair + 1) * 256].unsqueeze(1).to_broadcast([P, 2, 256]), op=ADD)
+
+        def s_tanh_u(b, qp, pair):
+            fin = pres["u", b, qp, pair]
+            nc.scalar.activation(out=fin[:], in_=fin[:], func=TANH)
+            nc.sync.dma_start(out=out[b, qp * 256:(qp + 1) * 256, pair * 256:(pair + 1) * 256].rearrange("(u p) c -> p u c", p=P),
+                              in_=fin[:].rearrange("p (u c) -> p u c", u=2))
+
+        def s_tanh(b, qb, pairs):
+            n = 256 * len(pairs)
+            lo = 256 * pairs[0]
+            fin = pres[b, qb, pairs[0]]
+            nc.scalar.activation(out=fin[:, 0:n], in_=fin[:, 0:n], func=TANH)
+            nc.sync.dma_start(out=out[b, qb * P:(qb + 1) * P, lo:lo + n], in_=fin[:, 0:n])
 
         nc.sync.dma_start(out=brow[0:1, :], in_=b_out.rearrange("(o n) -> o n", o=1))
         load_rows("a0", attn_weights[0], 0, 1)
@@ -206,8 +237,8 @@ def tile_attention_pb_kernel(tc, attn_weights, context, q, W_out, b_out, out):
         load_c_split(0, 1, 0)
         load_c_split(0, 1, 1)
         load_rows("q0", q[0], 0, 2)
-        load_rows("q0", q[0], 2, 2)
         load_w(0)
+        load_rows("q0", q[0], 2, 2)
         load_w(1)
         load_w(2)
         load_c_rows(1, 0)
@@ -261,37 +292,43 @@ def tile_attention_pb_kernel(tc, attn_weights, context, q, W_out, b_out, out):
 
         for qb in range(4):
             S1("s", 0, 0, qb)
-        for qb in range(4):
-            T_rows("s", "q", 0, qb)
-        for qb in range(4):
+        for qb in range(2):
+            T_rows("ss"[qb % 2], "q", 0, qb)
             Q_rows("q", 0, qb)
+        for Pp in range(4):
+            T_w("svsv"[Pp], 0, Pp)
+            if Pp % 2 == 1:
+                Q_w(0, Pp // 2)
         for qb in range(4):
-            S1("s", 0, 1, qb)
-        for qb in range(4):
+            S1("ssss"[qb], 0, 1, qb)
             Q_m(0, qb)
-        for pair in range(2):
-            for Pp in range(4):
-                T_w("sv"[Pp % 2], pair, Pp)
-                if Pp % 2 == 1:
-                    Q_w(pair, Pp // 2)
+        for qb in range(2, 4):
+            T_rows("ss"[qb % 2], "q", 0, qb)
+            Q_rows("q", 0, qb)
+        for Pp in range(4):
+            T_w("svsv"[Pp], 1, Pp)
+            if Pp % 2 == 1:
+                Q_w(1, Pp // 2)
 
+        def ctx1_regroup(g):
+            for G in range(2):
+                R_c("vsvs"[2 * G], 1, g, G, 0)
+                R_c("vsvs"[2 * G + 1], 1, g, G, 1)
+
+        ctx1_regroup(0)
         for pair in range(4):
-            for qb in range(4):
-                pe_S2(0, qb, pair)
-                if pair % 2 == 1:
-                    v_add(0, qb, pair // 2)
+            for qp in range(2):
+                pe_S2u(0, qp, pair)
+                v_add_u(0, qp, pair)
             if pair < 2:
-                for step in range(4):
-                    ctx1(pair, step)
+                Q_c(1, pair, 0)
+                Q_c(1, pair, 1)
                 for Pp in range(4):
                     T_w("s", pair + 2, Pp)
                 Q_w(pair + 2, 0)
                 Q_w(pair + 2, 1)
-                ctx1(pair, 4)
-                ctx1(pair, 5)
-            if pair == 1:
-                for qb in range(4):
-                    s_tanh(0, qb, 0)
+            if pair == 0:
+                ctx1_regroup(1)
             if pair == 2:
                 for qb in range(2):
                     T_rows("s", "a", 1, qb)
@@ -306,24 +343,24 @@ def tile_attention_pb_kernel(tc, attn_weights, context, q, W_out, b_out, out):
             Q_rows("q", 1, qb)
 
         def B(qb):
-            S1("s", 1, 0, qb)
+            S1("v", 1, 0, qb)
             S1("v", 1, 1, qb)
             Q_m(1, qb)
 
+        cuts = [[(0, 1), (2, 3)]] * 3 + [[(0, 1), (2,), (3,)]]
         B(0)
         for qb in range(4):
             if qb + 2 < 4:
                 A(qb + 2)
             if qb + 1 < 4:
                 B(qb + 1)
-            for i in range(4 if qb == 0 else 2):
-                if qb == 0:
-                    s_tanh(0, i, 1)
-                else:
-                    s_tanh(1, qb - 1, i)
-            for oh in range(2):
-                pe_S2(1, qb, 2 * oh)
-                pe_S2(1, qb, 2 * oh + 1)
-                v_add(1, qb, oh)
-        for oh in range(2):
-            s_tanh(1, 3, oh)
+            for qp in range(2):
+                s_tanh_u(0, qp, qb)
+            if qb > 0:
+                for pairs in cuts[qb - 1]:
+                    s_tanh(1, qb - 1, pairs)
+            for pairs in cuts[qb]:
+                pe_S2(1, qb, pairs)
+                v_add(1, qb, pairs)
+        for pairs in cuts[3]:
+            s_tanh(1, 3, pairs)

@@ -228,10 +228,10 @@ def tile_attention_pb_kernel(tc, attn_weights, context, q, W_out, b_out, out):
             nc.scalar.activation(out=fin[:, 0:n], in_=fin[:, 0:n], func=TANH)
             nc.sync.dma_start(out=out[b, qb * P:(qb + 1) * P, lo:lo + n], in_=fin[:, 0:n])
 
-        nc.sync.dma_start(out=brow[0:1, :], in_=b_out.rearrange("(o n) -> o n", o=1))
         load_rows("a0", attn_weights[0], 0, 1)
         load_c_split(0, 0, 0)
         load_c_split(0, 0, 1)
+        nc.sync.dma_start(out=brow[0:1, :], in_=b_out.rearrange("(o n) -> o n", o=1))
         load_rows("a0", attn_weights[0], 1, 1)
         load_rows("a0", attn_weights[0], 2, 2)
         load_c_split(0, 1, 0)
@@ -262,10 +262,6 @@ def tile_attention_pb_kernel(tc, attn_weights, context, q, W_out, b_out, out):
             else:
                 Q_c(1, g, step - 4)
 
-        for oh in range(2):
-            bb = ps_2.tile([P, 512], F32, name="bb", tag="s2")
-            nc.tensor.matmul(out=bb[:], lhsT=ones[:], rhs=brow[:, oh * 512:(oh + 1) * 512], start=True, stop=True)
-            nc.scalar.copy(out=bias[:, oh * 512:(oh + 1) * 512], in_=bb[:])
         T_rows("s", "a", 0, 0)
         for g in range(2):
             R_c("v", 0, g, 0, 0)
@@ -275,13 +271,17 @@ def tile_attention_pb_kernel(tc, attn_weights, context, q, W_out, b_out, out):
         Q_c(0, 1, 0)
         for qb in range(1, 4):
             T_rows("s", "a", 0, qb)
+        for oh in range(2):
+            bb = ps_2.tile([P, 512], F32, name="bb", tag="s2")
+            nc.tensor.matmul(out=bb[:], lhsT=ones[:], rhs=brow[:, oh * 512:(oh + 1) * 512], start=True, stop=True)
+            nc.scalar.copy(out=bias[:, oh * 512:(oh + 1) * 512], in_=bb[:])
         load_c_rows(1, 1)
         Q_rows("a", 0, 1)
         load_rows("a1", attn_weights[1], 0, 2)
         load_rows("a1", attn_weights[1], 2, 2)
         Q_rows("a", 0, 2)
-        R_c("v", 0, 0, 1, 0)
         Q_rows("a", 0, 3)
+        R_c("v", 0, 0, 1, 0)
         R_c("v", 0, 0, 1, 1)
         R_c("v", 0, 1, 1, 0)
         R_c("v", 0, 1, 1, 1)
@@ -330,7 +330,7 @@ def tile_attention_pb_kernel(tc, attn_weights, context, q, W_out, b_out, out):
             if pair == 0:
                 ctx1_regroup(1)
             if pair == 2:
-                for qb in range(2):
+                for qb in range(4):
                     T_rows("s", "a", 1, qb)
                     T_rows("s", "q", 1, qb)
                     Q_rows("a", 1, qb)
@@ -343,19 +343,21 @@ def tile_attention_pb_kernel(tc, attn_weights, context, q, W_out, b_out, out):
             Q_rows("q", 1, qb)
 
         def B(qb):
-            S1("v", 1, 0, qb)
+            S1("s", 1, 0, qb)
             S1("v", 1, 1, qb)
             Q_m(1, qb)
 
         cuts = [[(0, 1), (2, 3)]] * 3 + [[(0, 1), (2,), (3,)]]
-        B(0)
-        for qb in range(4):
-            if qb + 2 < 4:
-                A(qb + 2)
-            if qb + 1 < 4:
-                B(qb + 1)
+        def B_and_tanh(qb):
+            B(qb)
             for qp in range(2):
                 s_tanh_u(0, qp, qb)
+
+        B_and_tanh(0)
+        B_and_tanh(1)
+        for qb in range(4):
+            if qb + 2 < 4:
+                B_and_tanh(qb + 2)
             if qb > 0:
                 for pairs in cuts[qb - 1]:
                     s_tanh(1, qb - 1, pairs)

@@ -64,13 +64,17 @@ def tile_attention_pb_kernel(tc, attn_weights, context, q, W_out, b_out, out):
         def load_rows(key, src, first, blocks):
             if first == 0:
                 new_raw(key)
-            nc.sync.dma_start(out=raws[key][:, first * 1024:(first + blocks) * 1024].rearrange("p (r c) -> p r c", r=blocks),
-                              in_=src[first * P:(first + blocks) * P, :].rearrange("(r p) c -> p r c", p=P))
+            h = first // 2
+            rows = src[h * 256:(h + 1) * 256, :]
+            if blocks == 2:
+                nc.sync.dma_start(out=raws[key][:, first * 1024:(first + 2) * 1024], in_=rows.rearrange("(p r) c -> p (r c)", r=2))
+            else:
+                nc.sync.dma_start(out=raws[key][:, first * 1024:(first + 1) * 1024],
+                                  in_=rows.rearrange("(p r) c -> p r c", r=2)[:, first % 2])
 
         def load_w(pair):
             t = new_raw("w%d" % pair)
-            nc.sync.dma_start(out=t[:].rearrange("p (r c) -> p r c", r=2),
-                              in_=W_out[pair * 256:(pair + 1) * 256, :].rearrange("(r p) c -> p r c", p=P))
+            nc.sync.dma_start(out=t[:], in_=W_out[pair * 256:(pair + 1) * 256, :].rearrange("(p h) c -> p (h c)", h=2))
 
         def load_c_split(b, G, g):
             if g == 0:
@@ -168,7 +172,8 @@ def tile_attention_pb_kernel(tc, attn_weights, context, q, W_out, b_out, out):
             cp_words(eng, g_new((kind, b, qb), "ga", 4)[:], banks[kind, b, qb])
 
         def cp_w(eng, pair, Pp):
-            cp_words(eng, g_half(("w", pair, Pp // 2), "gw", 4, Pp % 2), banks["w", pair, Pp])
+            cp(eng)(out=g_half(("w", pair, Pp // 2), "gw", 4, Pp % 2).bitcast(F32).rearrange("p (o h u) -> p o h u", h=2, u=2),
+                    in_=banks["w", pair, Pp][:].rearrange("p (h u o) -> p o h u", h=2, u=2))
 
         def cp_m(eng, b, G, qb):
             if G == 0:
@@ -218,7 +223,7 @@ def tile_attention_pb_kernel(tc, attn_weights, context, q, W_out, b_out, out):
         def s_tanh_u(b, qp, pair):
             fin = pres["u", b, qp, pair]
             nc.scalar.activation(out=fin[:], in_=fin[:], func=TANH)
-            nc.sync.dma_start(out=out[b, qp * 256:(qp + 1) * 256, pair * 256:(pair + 1) * 256].rearrange("(u p) c -> p u c", p=P),
+            nc.sync.dma_start(out=out[b, qp * 256:(qp + 1) * 256, pair * 256:(pair + 1) * 256].rearrange("(p u) c -> p u c", u=2),
                               in_=fin[:].rearrange("p (u c) -> p u c", u=2))
 
         def s_tanh(b, qb, pairs):
@@ -226,7 +231,8 @@ def tile_attention_pb_kernel(tc, attn_weights, context, q, W_out, b_out, out):
             lo = 256 * pairs[0]
             fin = pres[b, qb, pairs[0]]
             nc.scalar.activation(out=fin[:, 0:n], in_=fin[:, 0:n], func=TANH)
-            nc.sync.dma_start(out=out[b, qb * P:(qb + 1) * P, lo:lo + n], in_=fin[:, 0:n])
+            h = qb // 2
+            nc.sync.dma_start(out=out[b, h * 256:(h + 1) * 256, lo:lo + n].rearrange("(p r) c -> p r c", r=2)[:, qb % 2], in_=fin[:, 0:n])
 
         load_rows("a0", attn_weights[0], 0, 1)
         load_c_split(0, 0, 0)
@@ -271,10 +277,6 @@ def tile_attention_pb_kernel(tc, attn_weights, context, q, W_out, b_out, out):
         Q_c(0, 1, 0)
         for qb in range(1, 4):
             T_rows("s", "a", 0, qb)
-        for oh in range(2):
-            bb = ps_2.tile([P, 512], F32, name="bb", tag="s2")
-            nc.tensor.matmul(out=bb[:], lhsT=ones[:], rhs=brow[:, oh * 512:(oh + 1) * 512], start=True, stop=True)
-            nc.scalar.copy(out=bias[:, oh * 512:(oh + 1) * 512], in_=bb[:])
         load_c_rows(1, 1)
         Q_rows("a", 0, 1)
         load_rows("a1", attn_weights[1], 0, 2)
@@ -295,6 +297,10 @@ def tile_attention_pb_kernel(tc, attn_weights, context, q, W_out, b_out, out):
         for qb in range(2):
             T_rows("ss"[qb % 2], "q", 0, qb)
             Q_rows("q", 0, qb)
+        for oh in range(2):
+            bb = ps_2.tile([P, 512], F32, name="bb", tag="s2")
+            nc.tensor.matmul(out=bb[:], lhsT=ones[:], rhs=brow[:, oh * 512:(oh + 1) * 512], start=True, stop=True)
+            nc.scalar.copy(out=bias[:, oh * 512:(oh + 1) * 512], in_=bb[:])
         for Pp in range(4):
             T_w("svsv"[Pp], 0, Pp)
             if Pp % 2 == 1:
@@ -329,10 +335,10 @@ def tile_attention_pb_kernel(tc, attn_weights, context, q, W_out, b_out, out):
                 Q_w(pair + 2, 1)
             if pair == 0:
                 ctx1_regroup(1)
-            if pair == 2:
-                for qb in range(4):
+            if pair >= 2:
+                for qb in range(2 * pair - 4, 2 * pair - 2):
                     T_rows("s", "a", 1, qb)
-                    T_rows("s", "q", 1, qb)
+                    T_rows("v", "q", 1, qb)
                     Q_rows("a", 1, qb)
                     Q_rows("q", 1, qb)
 

from contextlib import ExitStack

import concourse.mybir as mybir
from concourse.masks import make_identity

F32 = mybir.dt.float32
BF16 = mybir.dt.bfloat16
U32 = mybir.dt.uint32
U8 = mybir.dt.uint8
FP8X4 = mybir.dt.float8_e4m3fn_x4
TANH = mybir.ActivationFunctionType.Tanh
ADD = mybir.AluOpType.add

P = 128
FLOPS = 2 * 2 * 512 * 1024 * 1024 + 2 * 2 * 512 * 2048 * 1024


def tile_attention_pb_kernel(tc, attn_weights, context, q, W_out, b_out, out):
    nc = tc.nc
    with ExitStack() as ctx:
        ctx.enter_context(tc.manual_schedule())
        const = ctx.enter_context(tc.tile_pool(name="const", bufs=1))
        raw = ctx.enter_context(tc.tile_pool(name="raw", bufs=9))
        grp = ctx.enter_context(tc.tile_pool(name="grp", bufs=2))
        keep = ctx.enter_context(tc.tile_pool(name="keep", bufs=1))
        res = ctx.enter_context(tc.tile_pool(name="res", bufs=11))
        ps_a = ctx.enter_context(tc.psum_pool(name="ps_a", bufs=5))
        ps_2 = ctx.enter_context(tc.psum_pool(name="ps_2", bufs=3))

        ident = const.tile([P, P], F32, name="ident")
        make_identity(nc, ident[:])
        ones = const.tile([P, P], BF16, name="ones")
        nc.vector.memset(ones[:], 1.0)
        brow = const.tile([P, 1024], BF16, name="brow")
        nc.vector.memset(brow[:], 0.0)
        warm = const.tile([P, 8], F32, name="warm")
        nc.vector.memset(warm[:], 0.0)
        nc.scalar.activation(out=warm[:], in_=warm[:], func=TANH)
        bias = const.tile([P, 1024], F32, name="bias")

        def codes(name, width):
            c = keep.tile([P, width], U32, name=name + "_c", align_bytes=64)
            s = keep.tile([P, width], U8, name=name + "_s", align_bytes=64)
            return c, s

        a_q = [codes("a%d" % b, 1024) for b in range(2)]
        c_q = [codes("c%d" % b, 2048) for b in range(2)]
        q_q = [codes("q%d" % b, 1024) for b in range(2)]
        m_q = [codes("m%d" % b, 1024) for b in range(2)]
        w_q = codes("w", 4096)

        def quantise(dst, lo, src):
            n = src.shape[1] // 4
            nc.vector.quantize_mx(out=dst[0][:, lo:lo + n].bitcast(FP8X4), scales=dst[1][:, lo:lo + n], in_=src)

        raws = {}
        banks = {}
        g_tiles = {}

        def new_raw(key):
            raws[key] = raw.tile([P, 4096], BF16, name="raw_" + key, tag="raw")
            return raws[key]

        def load_rows(key, src, first, blocks):
            if first == 0:
                new_raw(key)
            h = first // 2
            rows = src[h * 256:(h + 1) * 256, :]
            if blocks == 2:
                nc.sync.dma_start(out=raws[key][:, first * 1024:(first + 2) * 1024], in_=rows.rearrange("(p r) c -> p (r c)", r=2))
            else:
                nc.sync.dma_start(out=raws[key][:, first * 1024:(first + 1) * 1024],
                                  in_=rows.rearrange("(p r) c -> p r c", r=2)[:, first % 2])

        def load_w(pair):
            t = new_raw("w%d" % pair)
            nc.sync.dma_start(out=t[:], in_=W_out[pair * 256:(pair + 1) * 256, :].rearrange("(p h) c -> p (h c)", h=2))

        def load_c_split(b, G, g):
            if g == 0:
                new_raw("c%d%d" % (b, G))
            t = raws["c%d%d" % (b, G)]
            for u in range(2):
                gu = 2 * g + u
                nc.sync.dma_start(
                    out=t[:, gu * 1024:(gu + 1) * 1024].rearrange("p (e f) -> p e f", e=2),
                    in_=context[b, gu * 256:(gu + 1) * 256, G * 512:(G + 1) * 512].rearrange("(p e) f -> p e f", e=2))

        def load_c_rows(b, g):
            t = new_raw("c%d%d" % (b, g))
            nc.sync.dma_start(out=t[:].rearrange("p (u x) -> p u x", u=2),
                              in_=context[b, g * 512:(g + 1) * 512, :].rearrange("(u p e) f -> p u (e f)", u=2, e=2))

        def c_src(b, g, G):
            if b == 0:
                return raws["c%d%d" % (b, G)][:].rearrange("p (g t f) -> p g t f", g=2, t=4)[:, g]
            return raws["c%d%d" % (b, g)][:].rearrange("p (t f) -> p t f", t=4)[:, :, G * 512:(G + 1) * 512]

        def pe_transposes(key, words, cols):
            bank = ps_a.tile([P, 512], F32, name="tp", tag="a")
            banks[key] = bank
            for i, c0 in enumerate(cols):
                nc.tensor.transpose(out=bank[:, i * P:(i + 1) * P], in_=words[:, c0:c0 + P], identity=ident[:])

        def pe_T_rows(kind, b, qb):
            pe_transposes((kind, b, qb), raws["%s%d" % (kind, b)][:].bitcast(F32), [qb * 512 + i * P for i in range(4)])

        def pe_T_w(pair, Pp):
            pe_transposes(("w", pair, Pp), raws["w%d" % pair][:].bitcast(F32),
                          [h * 1024 + Pp * 256 + u * P for h in range(2) for u in range(2)])

        def pe_S1(b, G, qb):
            bank = ps_a.tile([P, 512], F32, name="s1", tag="a")
            banks["m", b, G, qb] = bank
            for t2 in range(4):
                for g in range(2):
                    lo = g * 1024 + (4 * G + t2) * P
                    ro = (qb * 2 + g) * P
                    nc.tensor.matmul_mx(out=bank[:, t2 * P:(t2 + 1) * P],
                                        lhsT=c_q[b][0][:, lo:lo + P].bitcast(FP8X4), lhsT_scale=c_q[b][1][:, lo:lo + P],
                                        rhs=a_q[b][0][:, ro:ro + P].bitcast(FP8X4), rhs_scale=a_q[b][1][:, ro:ro + P],
                                        start=(g == 0), stop=(g == 1))

        def pe_S2(b, qb, pairs):
            bank = ps_2.tile([P, 512], F32, name="s2", tag="s2")
            banks["o", b, qb, pairs[0]] = bank
            for j, pair in enumerate(pairs):
                for i, Pp in enumerate((2, 3, 0, 1)):
                    if Pp < 2:
                        lc, lo = m_q[b], (qb * 2 + Pp) * P
                    else:
                        lc, lo = q_q[b], (qb * 2 + Pp - 2) * P
                    ro = pair * 1024 + Pp * 256
                    nc.tensor.matmul_mx(out=bank[:, j * 256:(j + 1) * 256],
                                        lhsT=lc[0][:, lo:lo + P].bitcast(FP8X4), lhsT_scale=lc[1][:, lo:lo + P],
                                        rhs=w_q[0][:, ro:ro + 256].bitcast(FP8X4), rhs_scale=w_q[1][:, ro:ro + 256],
                                        start=(i == 0), stop=(i == 3))

        def pe_S2u(b, qp, pair):
            bank = ps_2.tile([P, 512], F32, name="s2", tag="s2")
            banks["u", b, qp, pair] = bank
            for u in range(2):
                qb = 2 * qp + u
                for i, Pp in enumerate((2, 3, 0, 1)):
                    if Pp < 2:
                        lc, lo = m_q[b], (qb * 2 + Pp) * P
                    else:
                        lc, lo = q_q[b], (qb * 2 + Pp - 2) * P
                    ro = pair * 1024 + Pp * 256
                    nc.tensor.matmul_mx(out=bank[:, u * 256:(u + 1) * 256],
                                        lhsT=lc[0][:, lo:lo + P].bitcast(FP8X4), lhsT_scale=lc[1][:, lo:lo + P],
                                        rhs=w_q[0][:, ro:ro + 256].bitcast(FP8X4), rhs_scale=w_q[1][:, ro:ro + 256],
                                        start=(i == 0), stop=(i == 3))

        def cp(eng):
            return nc.scalar.copy if eng == "s" else nc.vector.tensor_copy

        def g_half(key, tag, bufs, half):
            if half == 0:
                g_tiles[key] = grp.tile([P, 2048], BF16, name="g" + tag, tag=tag, bufs=bufs, align_bytes=64)
            return g_tiles[key][:, half * 1024:(half + 1) * 1024]

        def g_new(key, tag, bufs):
            g_tiles[key] = grp.tile([P, 1024], BF16, name="g" + tag, tag=tag, bufs=bufs, align_bytes=64)
            return g_tiles[key]

        def cp_words(eng, dst, bank):
            cp(eng)(out=dst.bitcast(F32).rearrange("p (x r u) -> p x r u", x=2, u=2),
                    in_=bank[:].rearrange("p (x u r) -> p x r u", x=2, u=2))

        def cp_rows(eng, kind, b, qb):
            cp_words(eng, g_new((kind, b, qb), "ga", 4)[:], banks[kind, b, qb])

        def cp_w(eng, pair, Pp):
            cp(eng)(out=g_half(("w", pair, Pp // 2), "gw", 4, Pp % 2).bitcast(F32).rearrange("p (o h u) -> p o h u", h=2, u=2),
                    in_=banks["w", pair, Pp][:].rearrange("p (h u o) -> p o h u", h=2, u=2))

        def cp_m(eng, b, G, qb):
            if G == 0:
                g_new(("m", b, qb), "gm", 4)
            cp(eng)(out=g_tiles["m", b, qb][:, G * 512:(G + 1) * 512].rearrange("p (q t) -> p q t", t=4),
                    in_=banks["m", b, G, qb][:].rearrange("p (t q) -> p q t", t=4))

        def R_c(eng, b, g, G, ef):
            if ("c", b, g, G) not in g_tiles:
                g_tiles["c", b, g, G] = grp.tile([P, 2048], BF16, name="gc", tag="gc", bufs=4, align_bytes=64)
            gt = g_tiles["c", b, g, G]
            src = c_src(b, g, G)
            if eng == "s":
                nc.scalar.copy(out=gt[:].rearrange("p (J ef pp t) -> p J ef pp t", J=2, ef=2, t=4)[:, :, ef],
                               in_=src.rearrange("p t (J pp ef) -> p J ef pp t", J=2, ef=2)[:, :, ef])
            else:
                nc.vector.tensor_copy(out=gt[:].rearrange("p (J ef c i t) -> p J ef c t i", J=2, ef=2, i=4, t=4)[:, :, ef],
                                      in_=src.rearrange("p t (J c i ef) -> p J ef c t i", J=2, i=4, ef=2)[:, :, ef])

        def Q_rows(kind, b, qb):
            quantise(a_q[b] if kind == "a" else q_q[b], qb * 256, g_tiles[kind, b, qb][:])

        def Q_w(pair, half):
            quantise(w_q, pair * 1024 + half * 512, g_tiles["w", pair, half][:])

        def Q_c(b, g, G):
            quantise(c_q[b], g * 1024 + G * 512, g_tiles["c", b, g, G][:])

        def Q_m(b, qb):
            quantise(m_q[b], qb * 256, g_tiles["m", b, qb][:])

        pres = {}

        def v_add(b, qb, pairs):
            n = 256 * len(pairs)
            lo = 256 * pairs[0]
            pres[b, qb, pairs[0]] = res.tile([P, 512], F32, name="pre", tag="pre")
            nc.vector.tensor_tensor(out=pres[b, qb, pairs[0]][:, 0:n], in0=banks["o", b, qb, pairs[0]][:, 0:n],
                                    in1=bias[:, lo:lo + n], op=ADD)

        def v_add_u(b, qp, pair):
            pres["u", b, qp, pair] = res.tile([P, 512], F32, name="pre", tag="pre")
            nc.vector.tensor_tensor(out=pres["u", b, qp, pair][:].rearrange("p (u c) -> p u c", u=2),
                                    in0=banks["u", b, qp, pair][:].rearrange("p (u c) -> p u c", u=2),
                                    in1=bias[:, pair * 256:(pair + 1) * 256].unsqueeze(1).to_broadcast([P, 2, 256]), op=ADD)

        def s_tanh_u(b, qp, pair):
            fin = pres["u", b, qp, pair]
            nc.scalar.activation(out=fin[:], in_=fin[:], func=TANH)
            nc.sync.dma_start(out=out[b, qp * 256:(qp + 1) * 256, pair * 256:(pair + 1) * 256].rearrange("(p u) c -> p u c", u=2),
                              in_=fin[:].rearrange("p (u c) -> p u c", u=2))

        def s_tanh(b, qb, pairs):
            n = 256 * len(pairs)
            lo = 256 * pairs[0]
            fin = pres[b, qb, pairs[0]]
            nc.scalar.activation(out=fin[:, 0:n], in_=fin[:, 0:n], func=TANH)
            h = qb // 2
            nc.sync.dma_start(out=out[b, h * 256:(h + 1) * 256, lo:lo + n].rearrange("(p r) c -> p r c", r=2)[:, qb % 2], in_=fin[:, 0:n])

        load_rows("a0", attn_weights[0], 0, 1)
        load_c_split(0, 0, 0)
        load_c_split(0, 0, 1)
        nc.sync.dma_start(out=brow[0:1, :], in_=b_out.rearrange("(o n) -> o n", o=1))
        load_rows("a0", attn_weights[0], 1, 1)
        load_rows("a0", attn_weights[0], 2, 2)
        load_c_split(0, 1, 0)
        load_c_split(0, 1, 1)
        load_rows("q0", q[0], 0, 2)
        load_w(0)
        load_rows("q0", q[0], 2, 2)
        load_w(1)
        load_w(2)
        load_c_rows(1, 0)
        load_w(3)

        def T_rows(eng, kind, b, qb):
            pe_T_rows(kind, b, qb)
            cp_rows(eng, kind, b, qb)

        def T_w(eng, pair, Pp):
            pe_T_w(pair, Pp)
            cp_w(eng, pair, Pp)

        def S1(eng, b, G, qb):
            pe_S1(b, G, qb)
            cp_m(eng, b, G, qb)

        def ctx1(g, step):
            if step < 4:
                R_c("vs"[step % 2], 1, g, step // 2, step % 2)
            else:
                Q_c(1, g, step - 4)

        T_rows("s", "a", 0, 0)
        for g in range(2):
            R_c("v", 0, g, 0, 0)
            R_c("s", 0, g, 0, 1)
        Q_rows("a", 0, 0)
        Q_c(0, 0, 0)
        Q_c(0, 1, 0)
        for qb in range(1, 4):
            T_rows("s", "a", 0, qb)
        load_c_rows(1, 1)
        Q_rows("a", 0, 1)
        load_rows("a1", attn_weights[1], 0, 2)
        load_rows("a1", attn_weights[1], 2, 2)
        Q_rows("a", 0, 2)
        Q_rows("a", 0, 3)
        R_c("v", 0, 0, 1, 0)
        R_c("v", 0, 0, 1, 1)
        R_c("v", 0, 1, 1, 0)
        R_c("v", 0, 1, 1, 1)
        Q_c(0, 0, 1)
        Q_c(0, 1, 1)
        load_rows("q1", q[1], 0, 2)
        load_rows("q1", q[1], 2, 2)

        for qb in range(4):
            S1("s", 0, 0, qb)
        for qb in range(2):
            T_rows("ss"[qb % 2], "q", 0, qb)
            Q_rows("q", 0, qb)
        for oh in range(2):
            bb = ps_2.tile([P, 512], F32, name="bb", tag="s2")
            nc.tensor.matmul(out=bb[:], lhsT=ones[:], rhs=brow[:, oh * 512:(oh + 1) * 512], start=True, stop=True)
            nc.scalar.copy(out=bias[:, oh * 512:(oh + 1) * 512], in_=bb[:])
        for Pp in range(4):
            T_w("svsv"[Pp], 0, Pp)
            if Pp % 2 == 1:
                Q_w(0, Pp // 2)
        for qb in range(4):
            S1("ssss"[qb], 0, 1, qb)
            Q_m(0, qb)
        for qb in range(2, 4):
            T_rows("ss"[qb % 2], "q", 0, qb)
            Q_rows("q", 0, qb)
        for Pp in range(4):
            T_w("svsv"[Pp], 1, Pp)
            if Pp % 2 == 1:
                Q_w(1, Pp // 2)

        def ctx1_regroup(g):
            for G in range(2):
                R_c("vsvs"[2 * G], 1, g, G, 0)
                R_c("vsvs"[2 * G + 1], 1, g, G, 1)

        ctx1_regroup(0)
        for pair in range(4):
            for qp in range(2):
                pe_S2u(0, qp, pair)
                v_add_u(0, qp, pair)
            if pair < 2:
                Q_c(1, pair, 0)
                Q_c(1, pair, 1)
                for Pp in range(4):
                    T_w("s", pair + 2, Pp)
                Q_w(pair + 2, 0)
                Q_w(pair + 2, 1)
            if pair == 0:
                ctx1_regroup(1)
            if pair >= 2:
                for qb in range(2 * pair - 4, 2 * pair - 2):
                    T_rows("s", "a", 1, qb)
                    T_rows("v", "q", 1, qb)
                    Q_rows("a", 1, qb)
                    Q_rows("q", 1, qb)

        def A(qb):
            T_rows("s", "a", 1, qb)
            T_rows("s", "q", 1, qb)
            Q_rows("a", 1, qb)
            Q_rows("q", 1, qb)

        def B(qb):
            S1("s", 1, 0, qb)
            S1("v", 1, 1, qb)
            Q_m(1, qb)

        cuts = [[(0, 1), (2, 3)]] * 3 + [[(0, 1), (2,), (3,)]]
        def B_and_tanh(qb):
            B(qb)
            for qp in range(2):
                s_tanh_u(0, qp, qb)

        B_and_tanh(0)
        B_and_tanh(1)
        for qb in range(4):
            if qb + 2 < 4:
                B_and_tanh(qb + 2)
            if qb > 0:
                for pairs in cuts[qb - 1]:
                    s_tanh(1, qb - 1, pairs)
            for pairs in cuts[qb]:
                pe_S2(1, qb, pairs)
                v_add(1, qb, pairs)
        for pairs in cuts[3]:
            s_tanh(1, 3, pairs)
